import numpy as np
import ml_dtypes


def mxq(x, axis, fmt="e4m3"):
    dtype, down = {"e4m3": (ml_dtypes.float8_e4m3fn, 7), "e5m2": (ml_dtypes.float8_e5m2, 14)}[fmt]
    v = np.moveaxis(np.asarray(x, np.float32).astype(ml_dtypes.bfloat16).astype(np.float64), axis, -1)
    blocks = v.reshape(v.shape[:-1] + (-1, 32))
    amax = np.abs(blocks).max(-1, keepdims=True)
    byte = np.maximum(np.where(amax > 0, np.frexp(amax)[1] - 1 + 127, 0) - down, 1)
    scale = np.exp2(byte - 127.0)
    codes = (blocks / scale).astype(np.float32).astype(dtype).astype(np.float64)
    return np.moveaxis((codes * scale).reshape(v.shape), -1, axis)


WIDE = False


def mx_kscale(k):
    if not WIDE:
        return np.ones(k)
    levels = np.array([10, -10, 5, -5, 0])
    if k % 512:
        return np.exp2(np.random.permutation(np.resize(levels, k // 32))).repeat(32)
    a = np.empty((k // 512, 16))
    for p in range(k // 512):
        a[p, :8] = np.random.permutation(np.resize(levels, 8))
        for g in range(8):
            far = levels[np.abs(levels - a[p, g]) >= 10]
            a[p, g + 8] = far[np.random.randint(len(far))]
    return np.exp2(a.ravel()).repeat(32)


BF16 = ml_dtypes.bfloat16


def bf(x):
    return np.asarray(x, np.float32).astype(BF16)


def f64(x):
    return np.asarray(x).astype(np.float64)


B, H, NSE = 2048, 512, 1024


def sigmoid(v):
    return 1.0 / (1.0 + np.exp(-v))


def setup_inputs():
    s = mx_kscale(H)
    t = np.exp2(np.round(np.log2(mx_kscale(H)) / 2))
    return {"z_i": bf(np.random.standard_normal((B, H)) * (t * t)),
            "z_j": bf(np.random.standard_normal((B, H)) * s),
            "R": bf((np.eye(H) + np.random.standard_normal((H, H)) / np.sqrt(H)) / s[None, :]),
            "D": bf((1.0 + 0.3 * np.random.standard_normal((NSE, H))) * 0.9 / H ** 0.25 / t[None, :])}


def reference(z_i, z_j, R, D):
    Rz_j = f64(bf(mxq(f64(z_j), 1, "e4m3") @ mxq(f64(R), 1, "e4m3").T))
    p = f64(z_i) * Rz_j
    d2 = f64(D) * f64(D)
    scores = mxq(p, 1, "e4m3") @ mxq(d2, 1, "e4m3").T
    return sigmoid(scores)

@@ -1,0 +1,261 @@
+from contextlib import ExitStack
+
+import concourse.mybir as mybir
+from concourse.masks import make_identity
+
+B, H, NSE = 2048, 512, 1024
+FLOPS = 2 * B * H * H + 2 * B * H * NSE
+
+F32 = mybir.dt.float32
+BF16 = mybir.dt.bfloat16
+U32 = mybir.dt.uint32
+U8 = mybir.dt.uint8
+FP8X4 = mybir.dt.float8_e4m3fn_x4
+MULT = mybir.AluOpType.mult
+SIGMOID = mybir.ActivationFunctionType.Sigmoid
+SQUARE = mybir.ActivationFunctionType.Square
+
+P = 128
+QUADS = B // 512
+PAIRS = B // 256
+BANK_DT = BF16
+
+
+def tile_dedicomdecoder_kernel(tc, z_i, z_j, R, D, out):
+    nc = tc.nc
+    zj_v = z_j.rearrange("(c m f) k -> c m f k", m=P, f=4)
+    zi_v = z_i.rearrange("(c m f) k -> c m f k", m=P, f=4)
+    out_v = out.rearrange("(c m f) r -> c f m r", m=P, f=4)
+    r_v = R.rearrange("(q f) k -> q f k", f=4)
+    d_v = D.rearrange("(n a f) k -> n a f k", a=P, f=2)
+
+    with ExitStack() as ctx:
+        keep = ctx.enter_context(tc.tile_pool(name="keep", bufs=1))
+        work = ctx.enter_context(tc.tile_pool(name="work", bufs=3))
+        psum = ctx.enter_context(tc.psum_pool(name="psum", bufs=1))
+        ctx.enter_context(tc.manual_schedule())
+
+        def bank(tag, dtype=F32):
+            return psum.tile([P, 512], dtype, tag=tag, name=tag)
+
+        warm_sb = keep.tile([P, 512], BF16, tag="warm_sb", name="warm_sb")
+        nc.vector.memset(warm_sb[:], 0.0)
+        sig_in = keep.tile([P, 1], F32, tag="sig_in", name="sig_in")
+        nc.vector.memset(sig_in[:], 0.0)
+        sig_out = keep.tile([P, 1], F32, tag="sig_out", name="sig_out")
+        nc.scalar.activation(out=sig_out[:], in_=sig_in[:], func=SIGMOID)
+        ident = keep.tile([P, P], F32, tag="ident", name="ident")
+        make_identity(nc, ident[:])
+
+        r_sb = keep.tile([P, 4, H], BF16, tag="r_sb", name="r_sb")
+        zj_sb = [keep.tile([P, 4, H], BF16, tag="zj_sb%d" % c, name="zj_sb%d" % c) for c in range(QUADS)]
+        zi_sb = [keep.tile([P, 4, H], BF16, tag="zi_sb%d" % c, name="zi_sb%d" % c) for c in range(QUADS)]
+        d_sb = [keep.tile([P, 2, H], BF16, tag="d_sb%d" % n, name="d_sb%d" % n) for n in range(4)]
+        nc.sync.dma_start(out=r_sb[:], in_=r_v)
+        nc.sync.dma_start(out=d_sb[0][:], in_=d_v[0])
+        nc.sync.dma_start(out=d_sb[1][:], in_=d_v[1])
+        nc.sync.dma_start(out=zj_sb[0][:], in_=zj_v[0])
+        nc.sync.dma_start(out=d_sb[2][:], in_=d_v[2])
+        nc.sync.dma_start(out=d_sb[3][:], in_=d_v[3])
+        nc.sync.dma_start(out=zi_sb[0][:], in_=zi_v[0])
+        nc.sync.dma_start(out=zj_sb[1][:], in_=zj_v[1])
+        nc.sync.dma_start(out=zj_sb[2][:], in_=zj_v[2])
+        nc.sync.dma_start(out=zi_sb[1][:], in_=zi_v[1])
+        nc.sync.dma_start(out=zj_sb[3][:], in_=zj_v[3])
+        nc.sync.dma_start(out=zi_sb[2][:], in_=zi_v[2])
+        nc.sync.dma_start(out=zi_sb[3][:], in_=zi_v[3])
+
+        r_g = keep.tile([P, 4 * H], BF16, tag="r_g", name="r_g", align_bytes=64)
+        r_c = keep.tile([P, H], U32, tag="r_c", name="r_c", align_bytes=64)
+        r_s = keep.tile([P, H], U8, tag="r_s", name="r_s", align_bytes=64)
+        d2p = [keep.tile([P, 2, H], BF16, tag="d2p%d" % n, name="d2p%d" % n) for n in range(4)]
+        d2_g = [keep.tile([P, 2048], BF16, tag="d2_g%d" % h, name="d2_g%d" % h, align_bytes=64) for h in range(2)]
+        d2_c = [keep.tile([P, 512], U32, tag="d2_c%d" % h, name="d2_c%d" % h, align_bytes=64) for h in range(2)]
+        d2_s = [keep.tile([P, 512], U8, tag="d2_s%d" % h, name="d2_s%d" % h, align_bytes=64) for h in range(2)]
+        zj_g, zj_c, zj_s, p_sb, p_g, p_c, p_s, o_sb, banks = {}, {}, {}, {}, {}, {}, {}, {}, {}
+
+        warm_ps = bank("j3")
+
+        def warm(k):
+            for i in range(k):
+                nc.tensor.matmul(out=warm_ps[:], lhsT=warm_sb[:, 0:P], rhs=warm_sb[:], start=True, stop=True)
+
+        def transposes(key, tag, sources):
+            banks[key] = bank(tag)
+            for s, src in enumerate(sources):
+                nc.tensor.transpose(out=banks[key][:, s * P:(s + 1) * P], in_=src, identity=ident[:])
+
+        def copy_out(eng, dst, src):
+            if eng == "S":
+                nc.scalar.copy(out=dst, in_=src)
+            else:
+                nc.vector.tensor_copy(out=dst, in_=src)
+
+        def quantize(codes, scales, grouped):
+            nc.vector.quantize_mx(out=codes[:].bitcast(FP8X4), scales=scales[:], in_=grouped[:])
+
+        def every_2nd_word(rows, u):
+            return rows.bitcast(F32)[:, u:H // 2:2]
+
+        def word_block(rows, u):
+            return rows.bitcast(F32)[:, u * P:(u + 1) * P]
+
+        def perm_view(rows):
+            return rows.rearrange("p (q u e) -> p u q e", u=2, e=2)
+
+        def flat_view(rows):
+            return rows.rearrange("p (u q e) -> p u q e", u=2, e=2)
+
+        def RT(u):
+            transposes(("r", u), "e%d" % u, [every_2nd_word(r_sb[:, 2 * u + e, :], uk) for e in range(2) for uk in range(2)])
+
+        def RC(u, eng):
+            copy_out(eng, r_g[:, u * 1024:(u + 1) * 1024].bitcast(F32).rearrange("p (q s) -> p q s", s=4),
+                     banks[("r", u)][:].rearrange("p (s q) -> p q s", s=4))
+
+        def DS(n, eng="V"):
+            for f in range(2):
+                if eng == "V":
+                    nc.vector.tensor_tensor(out=flat_view(d2p[n][:, f, :]), in0=perm_view(d_sb[n][:, f, :]), in1=perm_view(d_sb[n][:, f, :]), op=MULT)
+                else:
+                    nc.scalar.activation(out=flat_view(d2p[n][:, f, :]), in_=perm_view(d_sb[n][:, f, :]), func=SQUARE)
+
+        def DT(n):
+            transposes(("d", n), "j%d" % n, [word_block(d2p[n][:, f, :], u) for f in range(2) for u in range(2)])
+
+        def DC(n, eng):
+            copy_out(eng, d2_g[n // 2][:, (n % 2) * 1024:(n % 2 + 1) * 1024].bitcast(F32).rearrange("p (a s) -> p a s", s=4),
+                     banks[("d", n)][:].rearrange("p (s a) -> p a s", s=4))
+
+        def DTr(n):
+            transposes(("d", n), "j%d" % n, [every_2nd_word(d_sb[n][:, f, :], u) for f in range(2) for u in range(2)])
+
+        def DCs(n):
+            nc.scalar.activation(out=d2_g[n // 2][:, (n % 2) * 1024:(n % 2 + 1) * 1024].rearrange("p (a s e) -> p a s e", s=4, e=2),
+                                 in_=banks[("d", n)][:].bitcast(BF16).rearrange("p (s a e) -> p a s e", s=4, e=2), func=SQUARE)
+
+        def DQ(h):
+            quantize(d2_c[h], d2_s[h], d2_g[h])
+
+        def pair_copy(eng, grouped, bk):
+            copy_out(eng, grouped[:].bitcast(F32).rearrange("p (t m u) -> p t m u", t=2, u=2),
+                     bk[:].rearrange("p (t u m) -> p t m u", t=2, u=2))
+
+        def A(g, tag="tA"):
+            c, fb = divmod(g, 2)
+            transposes(("a", g), tag, [every_2nd_word(zj_sb[c][:, 2 * fb + t, :], uk) for t in range(2) for uk in range(2)])
+
+        def Bc(g, eng):
+            zj_g[g] = work.tile([P, 1024], BF16, tag="zj_g", name="zj_g", bufs=PAIRS, align_bytes=64)
+            pair_copy(eng, zj_g[g], banks[("a", g)])
+
+        def Cq(g):
+            zj_c[g] = work.tile([P, 256], U32, tag="zj_c", name="zj_c", bufs=PAIRS, align_bytes=64)
+            zj_s[g] = work.tile([P, 256], U8, tag="zj_s", name="zj_s", bufs=PAIRS, align_bytes=64)
+            quantize(zj_c[g], zj_s[g], zj_g[g])
+
+        def E(t, tag=None):
+            g, et = divmod(t, 2)
+            cols = slice(et * P, (et + 1) * P)
+            banks[("e", t)] = bank(tag or "e%d" % et, BANK_DT)
+            nc.tensor.matmul_mx(out=banks[("e", t)][:], lhsT=zj_c[g][:, cols].bitcast(FP8X4), lhsT_scale=zj_s[g][:, cols],
+                                rhs=r_c[:].bitcast(FP8X4), rhs_scale=r_s[:], start=True, stop=True)
+
+        def Fm(t):
+            g, et = divmod(t, 2)
+            c, f = divmod(t, 4)
+            if et == 0:
+                p_sb[g] = work.tile([P, 2, H], BF16, tag="p_sb", name="p_sb")
+            nc.vector.tensor_tensor(out=flat_view(p_sb[g][:, et, :]), in0=flat_view(banks[("e", t)][:]), in1=perm_view(zi_sb[c][:, f, :]), op=MULT)
+
+        def G(g):
+            transposes(("g", g), "tG", [word_block(p_sb[g][:, t, :], u) for t in range(2) for u in range(2)])
+
+        def Hc(g, eng):
+            p_g[g] = work.tile([P, 1024], BF16, tag="p_g", name="p_g", align_bytes=64)
+            pair_copy(eng, p_g[g], banks[("g", g)])
+
+        def Iq(g):
+            p_c[g] = work.tile([P, 256], U32, tag="p_c", name="p_c", align_bytes=64)
+            p_s[g] = work.tile([P, 256], U8, tag="p_s", name="p_s", align_bytes=64)
+            quantize(p_c[g], p_s[g], p_g[g])
+
+        def J(t):
+            g, et = divmod(t, 2)
+            cols = slice(et * P, (et + 1) * P)
+            for n in range(2):
+                banks[("j", t, n)] = bank("j%d" % ((2 * t + n) % 4))
+                nc.tensor.matmul_mx(out=banks[("j", t, n)][:], lhsT=p_c[g][:, cols].bitcast(FP8X4), lhsT_scale=p_s[g][:, cols],
+                                    rhs=d2_c[n][:].bitcast(FP8X4), rhs_scale=d2_s[n][:], start=True, stop=True)
+
+        def K(t):
+            c, f = divmod(t, 4)
+            o_sb[t] = work.tile([P, NSE], F32, tag="o_sb", name="o_sb", bufs=6)
+            for n in range(2):
+                half = slice(n * 512, (n + 1) * 512)
+                nc.scalar.activation(out=o_sb[t][:, half], in_=banks[("j", t, n)][:], func=SIGMOID)
+                if t == 2 * PAIRS - 1:
+                    nc.sync.dma_start(out=out_v[c, f][:, half], in_=o_sb[t][:, half])
+            if t < 2 * PAIRS - 1:
+                nc.sync.dma_start(out=out_v[c, f], in_=o_sb[t][:])
+
+        warm(6)
+        RT(0); RT(1)
+        RC(0, "S"); RC(1, "S")
+        DS(0); DS(1)
+        DT(0); DT(1)
+        DC(0, "S"); DC(1, "S")
+        quantize(r_c, r_s, r_g)
+        warm(2)
+        A(0, "tA"); A(1, "tG")
+        Bc(0, "S"); Bc(1, "S")
+        DS(2)
+        DQ(0)
+        Cq(0)
+        DT(2); DC(2, "S")
+        E(0); E(1)
+        DS(3)
+        Cq(1)
+        DT(3); DC(3, "S")
+        E(2, "j0"); E(3, "j1")
+        Fm(0); Fm(1)
+        G(0)
+        Hc(0, "S")
+        A(2, "tA")
+        Bc(2, "S")
+        Fm(2); Fm(3)
+        G(1)
+        Hc(1, "S")
+        A(3, "e1")
+        Bc(3, "S")
+        DQ(1)
+        Iq(0)
+        Cq(2)
+        Iq(1)
+        J(0); J(1)
+        E(4); E(5)
+        K(0); K(1)
+        extras = {1: ((4, "tA"),), 2: ((5, "tA"),), 3: ((6, "tA"),), 4: ((7, "tA"),)}
+        for s in range(1, PAIRS + 1):
+            if s < PAIRS and s >= 2:
+                G(s)
+            for g, tag in extras.get(s, ()):
+                A(g, tag)
+            if s + 1 < PAIRS and s + 1 >= 2:
+                Fm(2 * s + 2)
+            if s < PAIRS and s >= 2:
+                Hc(s, "V")
+            if s + 2 < PAIRS and s + 2 >= 3:
+                Cq(s + 2)
+            if s + 1 < PAIRS and s + 1 >= 2:
+                Fm(2 * s + 3)
+            if s < PAIRS and s >= 2:
+                Iq(s)
+            for g, tag in extras.get(s, ()):
+                Bc(g, "S")
+            if s - 1 >= 1:
+                J(2 * s - 2); J(2 * s - 1)
+            if s + 2 < PAIRS and s + 2 >= 3:
+                E(2 * s + 4); E(2 * s + 5)
+            if s - 1 >= 1:
+                K(2 * s - 2); K(2 * s - 1)

@@ -72,7 +72,7 @@ def tile_dedicomdecoder_kernel(tc, z_i, z_j, R, D, out):
         d2_g = [keep.tile([P, 2048], BF16, tag="d2_g%d" % h, name="d2_g%d" % h, align_bytes=64) for h in range(2)]
         d2_c = [keep.tile([P, 512], U32, tag="d2_c%d" % h, name="d2_c%d" % h, align_bytes=64) for h in range(2)]
         d2_s = [keep.tile([P, 512], U8, tag="d2_s%d" % h, name="d2_s%d" % h, align_bytes=64) for h in range(2)]
-        zj_g, zj_c, zj_s, p_sb, p_g, p_c, p_s, o_sb, banks = {}, {}, {}, {}, {}, {}, {}, {}, {}
+        zj_p, zj_g, zj_c, zj_s, p_sb, p_g, p_c, p_s, o_sb, banks = {}, {}, {}, {}, {}, {}, {}, {}, {}, {}
 
         warm_ps = bank("j3")
 
@@ -145,6 +145,15 @@ def tile_dedicomdecoder_kernel(tc, z_i, z_j, R, D, out):
             c, fb = divmod(g, 2)
             transposes(("a", g), tag, [every_2nd_word(zj_sb[c][:, 2 * fb + t, :], uk) for t in range(2) for uk in range(2)])
 
+        def Pp(g):
+            c, fb = divmod(g, 2)
+            zj_p[g] = work.tile([P, 2, H], BF16, tag="zj_p", name="zj_p", bufs=3)
+            nc.vector.tensor_copy(out=zj_p[g][:].bitcast(F32).rearrange("p t (u q) -> p t u q", u=2),
+                                  in_=zj_sb[c][:, 2 * fb:2 * fb + 2, :].bitcast(F32).rearrange("p t (q u) -> p t u q", u=2))
+
+        def Ac(g, tag="tA"):
+            transposes(("a", g), tag, [word_block(zj_p[g][:, t, :], uk) for t in range(2) for uk in range(2)])
+
         def Bc(g, eng):
             zj_g[g] = work.tile([P, 1024], BF16, tag="zj_g", name="zj_g", bufs=PAIRS, align_bytes=64)
             pair_copy(eng, zj_g[g], banks[("a", g)])
@@ -202,28 +211,29 @@ def tile_dedicomdecoder_kernel(tc, z_i, z_j, R, D, out):
         warm(6)
         RT(0); RT(1)
         RC(0, "S"); RC(1, "S")
+        warm(2)
         DS(0); DS(1)
         DT(0); DT(1)
         DC(0, "S"); DC(1, "S")
         quantize(r_c, r_s, r_g)
-        warm(2)
         A(0, "tA"); A(1, "tG")
         Bc(0, "S"); Bc(1, "S")
+        warm(2)
         DS(2)
-        DQ(0)
         Cq(0)
         DT(2); DC(2, "S")
         E(0); E(1)
         DS(3)
         Cq(1)
         DT(3); DC(3, "S")
-        E(2, "j0"); E(3, "j1")
         Fm(0); Fm(1)
         G(0)
         Hc(0, "S")
+        E(2, "j0"); E(3, "j1")
+        DQ(0)
+        Fm(2); Fm(3)
         A(2, "tA")
         Bc(2, "S")
-        Fm(2); Fm(3)
         G(1)
         Hc(1, "S")
         A(3, "e1")
@@ -232,15 +242,15 @@ def tile_dedicomdecoder_kernel(tc, z_i, z_j, R, D, out):
         Iq(0)
         Cq(2)
         Iq(1)
+        Pp(4)
         J(0); J(1)
         E(4); E(5)
         K(0); K(1)
-        extras = {1: ((4, "tA"),), 2: ((5, "tA"),), 3: ((6, "tA"),), 4: ((7, "tA"),)}
         for s in range(1, PAIRS + 1):
             if s < PAIRS and s >= 2:
                 G(s)
-            for g, tag in extras.get(s, ()):
-                A(g, tag)
+            if 4 <= s + 3 < PAIRS:
+                Ac(s + 3)
             if s + 1 < PAIRS and s + 1 >= 2:
                 Fm(2 * s + 2)
             if s < PAIRS and s >= 2:
@@ -251,8 +261,10 @@ def tile_dedicomdecoder_kernel(tc, z_i, z_j, R, D, out):
                 Fm(2 * s + 3)
             if s < PAIRS and s >= 2:
                 Iq(s)
-            for g, tag in extras.get(s, ()):
-                Bc(g, "S")
+            if 4 <= s + 3 < PAIRS:
+                Bc(s + 3, "V")
+            if s + 4 < PAIRS:
+                Pp(s + 4)
             if s - 1 >= 1:
                 J(2 * s - 2); J(2 * s - 1)
             if s + 2 < PAIRS and s + 2 >= 3:

@@ -13,21 +13,44 @@ U8 = mybir.dt.uint8
 FP8X4 = mybir.dt.float8_e4m3fn_x4
 MULT = mybir.AluOpType.mult
 SIGMOID = mybir.ActivationFunctionType.Sigmoid
-SQUARE = mybir.ActivationFunctionType.Square
 
 P = 128
-QUADS = B // 512
-PAIRS = B // 256
-BANK_DT = BF16
+WORDS = H // 2
+QUADS = B // (4 * P)
+PAIRS = B // (2 * P)
+LAST_TILE = B // P - 1
+D_GROUPS = NSE // (2 * P)
+BANK_COLS = 512
+STAGE1_PSUM = BF16
+PAIR_COLS = 2 * P
+FIRST_REORDERED_PAIR = 3
+WARM_UP_MATMULS = 6
+KEEP_UP_MATMULS = 2
+
+
+def every_second_word(row_tile, u):
+    return row_tile.bitcast(F32)[:, u:WORDS:2]
+
+
+def word_run(row_tile, u):
+    return row_tile.bitcast(F32)[:, u * P:(u + 1) * P]
+
+
+def stepped_in_transpose_order(row_tile):
+    return row_tile.rearrange("part (q u e) -> part u q e", u=2, e=2)
+
+
+def stored_in_transpose_order(row_tile):
+    return row_tile.rearrange("part (u q e) -> part u q e", u=2, e=2)
 
 
 def tile_dedicomdecoder_kernel(tc, z_i, z_j, R, D, out):
     nc = tc.nc
-    zj_v = z_j.rearrange("(c m f) k -> c m f k", m=P, f=4)
-    zi_v = z_i.rearrange("(c m f) k -> c m f k", m=P, f=4)
-    out_v = out.rearrange("(c m f) r -> c f m r", m=P, f=4)
-    r_v = R.rearrange("(q f) k -> q f k", f=4)
-    d_v = D.rearrange("(n a f) k -> n a f k", a=P, f=2)
+    zj_quads = z_j.rearrange("(c m f) k -> c m f k", m=P, f=4)
+    zi_quads = z_i.rearrange("(c m f) h -> c m f h", m=P, f=4)
+    out_tiles = out.rearrange("(c m f) r -> c f m r", m=P, f=4)
+    r_rows = R.rearrange("(q f) k -> q f k", f=4)
+    d_groups = D.rearrange("(n a f) h -> n a f h", a=P, f=2)
 
     with ExitStack() as ctx:
         keep = ctx.enter_context(tc.tile_pool(name="keep", bufs=1))
@@ -36,238 +59,230 @@ def tile_dedicomdecoder_kernel(tc, z_i, z_j, R, D, out):
         ctx.enter_context(tc.manual_schedule())
 
         def bank(tag, dtype=F32):
-            return psum.tile([P, 512], dtype, tag=tag, name=tag)
+            return psum.tile([P, BANK_COLS], dtype, tag=tag, name=tag)
 
-        warm_sb = keep.tile([P, 512], BF16, tag="warm_sb", name="warm_sb")
-        nc.vector.memset(warm_sb[:], 0.0)
-        sig_in = keep.tile([P, 1], F32, tag="sig_in", name="sig_in")
-        nc.vector.memset(sig_in[:], 0.0)
-        sig_out = keep.tile([P, 1], F32, tag="sig_out", name="sig_out")
-        nc.scalar.activation(out=sig_out[:], in_=sig_in[:], func=SIGMOID)
-        ident = keep.tile([P, P], F32, tag="ident", name="ident")
-        make_identity(nc, ident[:])
+        zeros = keep.tile([P, BANK_COLS], BF16, tag="zeros", name="zeros")
+        nc.vector.memset(zeros[:], 0.0)
+        table_in = keep.tile([P, 1], F32, tag="table_in", name="table_in")
+        nc.vector.memset(table_in[:], 0.0)
+        table_out = keep.tile([P, 1], F32, tag="table_out", name="table_out")
+        nc.scalar.activation(out=table_out[:], in_=table_in[:], func=SIGMOID)
+        identity = keep.tile([P, P], F32, tag="identity", name="identity")
+        make_identity(nc, identity[:])
 
         r_sb = keep.tile([P, 4, H], BF16, tag="r_sb", name="r_sb")
+        d_sb = [keep.tile([P, 2, H], BF16, tag="d_sb%d" % n, name="d_sb%d" % n) for n in range(D_GROUPS)]
         zj_sb = [keep.tile([P, 4, H], BF16, tag="zj_sb%d" % c, name="zj_sb%d" % c) for c in range(QUADS)]
         zi_sb = [keep.tile([P, 4, H], BF16, tag="zi_sb%d" % c, name="zi_sb%d" % c) for c in range(QUADS)]
-        d_sb = [keep.tile([P, 2, H], BF16, tag="d_sb%d" % n, name="d_sb%d" % n) for n in range(4)]
-        nc.sync.dma_start(out=r_sb[:], in_=r_v)
-        nc.sync.dma_start(out=d_sb[0][:], in_=d_v[0])
-        nc.sync.dma_start(out=d_sb[1][:], in_=d_v[1])
-        nc.sync.dma_start(out=zj_sb[0][:], in_=zj_v[0])
-        nc.sync.dma_start(out=d_sb[2][:], in_=d_v[2])
-        nc.sync.dma_start(out=d_sb[3][:], in_=d_v[3])
-        nc.sync.dma_start(out=zi_sb[0][:], in_=zi_v[0])
-        nc.sync.dma_start(out=zj_sb[1][:], in_=zj_v[1])
-        nc.sync.dma_start(out=zj_sb[2][:], in_=zj_v[2])
-        nc.sync.dma_start(out=zi_sb[1][:], in_=zi_v[1])
-        nc.sync.dma_start(out=zj_sb[3][:], in_=zj_v[3])
-        nc.sync.dma_start(out=zi_sb[2][:], in_=zi_v[2])
-        nc.sync.dma_start(out=zi_sb[3][:], in_=zi_v[3])
 
-        r_g = keep.tile([P, 4 * H], BF16, tag="r_g", name="r_g", align_bytes=64)
-        r_c = keep.tile([P, H], U32, tag="r_c", name="r_c", align_bytes=64)
-        r_s = keep.tile([P, H], U8, tag="r_s", name="r_s", align_bytes=64)
-        d2p = [keep.tile([P, 2, H], BF16, tag="d2p%d" % n, name="d2p%d" % n) for n in range(4)]
-        d2_g = [keep.tile([P, 2048], BF16, tag="d2_g%d" % h, name="d2_g%d" % h, align_bytes=64) for h in range(2)]
-        d2_c = [keep.tile([P, 512], U32, tag="d2_c%d" % h, name="d2_c%d" % h, align_bytes=64) for h in range(2)]
-        d2_s = [keep.tile([P, 512], U8, tag="d2_s%d" % h, name="d2_s%d" % h, align_bytes=64) for h in range(2)]
-        zj_p, zj_g, zj_c, zj_s, p_sb, p_g, p_c, p_s, o_sb, banks = {}, {}, {}, {}, {}, {}, {}, {}, {}, {}
+        def load_d(n):
+            nc.sync.dma_start(out=d_sb[n][:], in_=d_groups[n])
 
-        warm_ps = bank("j3")
+        def load_zj(c):
+            nc.sync.dma_start(out=zj_sb[c][:], in_=zj_quads[c])
 
-        def warm(k):
-            for i in range(k):
-                nc.tensor.matmul(out=warm_ps[:], lhsT=warm_sb[:, 0:P], rhs=warm_sb[:], start=True, stop=True)
+        def load_zi(c):
+            nc.sync.dma_start(out=zi_sb[c][:], in_=zi_quads[c])
 
-        def transposes(key, tag, sources):
+        nc.sync.dma_start(out=r_sb[:], in_=r_rows)
+        load_d(0)
+        load_d(1)
+        load_zj(0)
+        load_d(2)
+        load_d(3)
+        load_zi(0)
+        load_zj(1)
+        load_zj(2)
+        load_zi(1)
+        load_zj(3)
+        load_zi(2)
+        load_zi(3)
+
+        r_grouped = keep.tile([P, 4 * H], BF16, tag="r_grouped", name="r_grouped", align_bytes=64)
+        r_codes = keep.tile([P, H], U32, tag="r_codes", name="r_codes", align_bytes=64)
+        r_scales = keep.tile([P, H], U8, tag="r_scales", name="r_scales", align_bytes=64)
+        dd_sb = [keep.tile([P, 2, H], BF16, tag="dd_sb%d" % n, name="dd_sb%d" % n) for n in range(D_GROUPS)]
+        dd_grouped = [keep.tile([P, 4 * BANK_COLS], BF16, tag="dd_grouped%d" % half, name="dd_grouped%d" % half, align_bytes=64)
+                      for half in range(2)]
+        dd_codes = [keep.tile([P, BANK_COLS], U32, tag="dd_codes%d" % half, name="dd_codes%d" % half, align_bytes=64)
+                    for half in range(2)]
+        dd_scales = [keep.tile([P, BANK_COLS], U8, tag="dd_scales%d" % half, name="dd_scales%d" % half, align_bytes=64)
+                     for half in range(2)]
+        banks, zj_ordered, zj_grouped, zj_codes, zj_scales = {}, {}, {}, {}, {}
+        p_sb, p_grouped, p_codes, p_scales = {}, {}, {}, {}
+
+        idle_bank = bank("stage2_3")
+
+        def keep_tensor_clock_up(count):
+            for repeat in range(count):
+                nc.tensor.matmul(out=idle_bank[:], lhsT=zeros[:, 0:P], rhs=zeros[:], start=True, stop=True)
+
+        def transpose_four(key, tag, sources):
             banks[key] = bank(tag)
-            for s, src in enumerate(sources):
-                nc.tensor.transpose(out=banks[key][:, s * P:(s + 1) * P], in_=src, identity=ident[:])
-
-        def copy_out(eng, dst, src):
-            if eng == "S":
-                nc.scalar.copy(out=dst, in_=src)
-            else:
-                nc.vector.tensor_copy(out=dst, in_=src)
+            for slot, source in enumerate(sources):
+                nc.tensor.transpose(out=banks[key][:, slot * P:(slot + 1) * P], in_=source, identity=identity[:])
 
         def quantize(codes, scales, grouped):
             nc.vector.quantize_mx(out=codes[:].bitcast(FP8X4), scales=scales[:], in_=grouped[:])
 
-        def every_2nd_word(rows, u):
-            return rows.bitcast(F32)[:, u:H // 2:2]
+        def transpose_r(u):
+            transpose_four(("r", u), "stage1_%d" % u,
+                           [every_second_word(r_sb[:, 2 * u + e, :], v) for e in range(2) for v in range(2)])
 
-        def word_block(rows, u):
-            return rows.bitcast(F32)[:, u * P:(u + 1) * P]
+        def copy_r(u):
+            nc.scalar.copy(out=r_grouped[:, u * 2 * H:(u + 1) * 2 * H].bitcast(F32).rearrange("part (q slot) -> part q slot", slot=4),
+                           in_=banks[("r", u)][:].rearrange("part (slot q) -> part q slot", slot=4))
 
-        def perm_view(rows):
-            return rows.rearrange("p (q u e) -> p u q e", u=2, e=2)
-
-        def flat_view(rows):
-            return rows.rearrange("p (u q e) -> p u q e", u=2, e=2)
-
-        def RT(u):
-            transposes(("r", u), "e%d" % u, [every_2nd_word(r_sb[:, 2 * u + e, :], uk) for e in range(2) for uk in range(2)])
-
-        def RC(u, eng):
-            copy_out(eng, r_g[:, u * 1024:(u + 1) * 1024].bitcast(F32).rearrange("p (q s) -> p q s", s=4),
-                     banks[("r", u)][:].rearrange("p (s q) -> p q s", s=4))
-
-        def DS(n, eng="V"):
+        def square_d(n):
             for f in range(2):
-                if eng == "V":
-                    nc.vector.tensor_tensor(out=flat_view(d2p[n][:, f, :]), in0=perm_view(d_sb[n][:, f, :]), in1=perm_view(d_sb[n][:, f, :]), op=MULT)
-                else:
-                    nc.scalar.activation(out=flat_view(d2p[n][:, f, :]), in_=perm_view(d_sb[n][:, f, :]), func=SQUARE)
+                d_rows = stepped_in_transpose_order(d_sb[n][:, f, :])
+                nc.vector.tensor_tensor(out=stored_in_transpose_order(dd_sb[n][:, f, :]), in0=d_rows, in1=d_rows, op=MULT)
 
-        def DT(n):
-            transposes(("d", n), "j%d" % n, [word_block(d2p[n][:, f, :], u) for f in range(2) for u in range(2)])
+        def transpose_d(n):
+            transpose_four(("d", n), "stage2_%d" % n, [word_run(dd_sb[n][:, f, :], u) for f in range(2) for u in range(2)])
 
-        def DC(n, eng):
-            copy_out(eng, d2_g[n // 2][:, (n % 2) * 1024:(n % 2 + 1) * 1024].bitcast(F32).rearrange("p (a s) -> p a s", s=4),
-                     banks[("d", n)][:].rearrange("p (s a) -> p a s", s=4))
+        def copy_d(n):
+            cols = slice((n % 2) * 2 * BANK_COLS, (n % 2 + 1) * 2 * BANK_COLS)
+            nc.scalar.copy(out=dd_grouped[n // 2][:, cols].bitcast(F32).rearrange("part (a slot) -> part a slot", slot=4),
+                           in_=banks[("d", n)][:].rearrange("part (slot a) -> part a slot", slot=4))
 
-        def DTr(n):
-            transposes(("d", n), "j%d" % n, [every_2nd_word(d_sb[n][:, f, :], u) for f in range(2) for u in range(2)])
+        def quantize_d(half):
+            quantize(dd_codes[half], dd_scales[half], dd_grouped[half])
 
-        def DCs(n):
-            nc.scalar.activation(out=d2_g[n // 2][:, (n % 2) * 1024:(n % 2 + 1) * 1024].rearrange("p (a s e) -> p a s e", s=4, e=2),
-                                 in_=banks[("d", n)][:].bitcast(BF16).rearrange("p (s a e) -> p a s e", s=4, e=2), func=SQUARE)
+        def copy_pair(on_scalar, grouped, pair_bank):
+            columns = grouped[:].bitcast(F32).rearrange("part (x m u) -> part x m u", x=2, u=2)
+            slots = pair_bank[:].rearrange("part (x u m) -> part x m u", x=2, u=2)
+            if on_scalar:
+                nc.scalar.copy(out=columns, in_=slots)
+            else:
+                nc.vector.tensor_copy(out=columns, in_=slots)
 
-        def DQ(h):
-            quantize(d2_c[h], d2_s[h], d2_g[h])
+        def reorder_zj(g):
+            c, first = g // 2, 2 * (g % 2)
+            zj_ordered[g] = work.tile([P, 2, H], BF16, tag="zj_ordered", name="zj_ordered")
+            nc.vector.tensor_copy(out=zj_ordered[g][:].bitcast(F32).rearrange("part x (u q) -> part x u q", u=2),
+                                  in_=zj_sb[c][:, first:first + 2, :].bitcast(F32).rearrange("part x (q u) -> part x u q", u=2))
 
-        def pair_copy(eng, grouped, bk):
-            copy_out(eng, grouped[:].bitcast(F32).rearrange("p (t m u) -> p t m u", t=2, u=2),
-                     bk[:].rearrange("p (t u m) -> p t m u", t=2, u=2))
+        def transpose_zj(g, tag="zjT"):
+            c, first = g // 2, 2 * (g % 2)
+            if g >= FIRST_REORDERED_PAIR:
+                sources = [word_run(zj_ordered[g][:, x, :], u) for x in range(2) for u in range(2)]
+            else:
+                sources = [every_second_word(zj_sb[c][:, first + x, :], u) for x in range(2) for u in range(2)]
+            transpose_four(("zj", g), tag, sources)
 
-        def A(g, tag="tA"):
-            c, fb = divmod(g, 2)
-            transposes(("a", g), tag, [every_2nd_word(zj_sb[c][:, 2 * fb + t, :], uk) for t in range(2) for uk in range(2)])
+        def copy_zj(g):
+            zj_grouped[g] = work.tile([P, 4 * PAIR_COLS], BF16, tag="zj_grouped", name="zj_grouped", align_bytes=64)
+            copy_pair(True, zj_grouped[g], banks[("zj", g)])
 
-        def Pp(g):
-            c, fb = divmod(g, 2)
-            zj_p[g] = work.tile([P, 2, H], BF16, tag="zj_p", name="zj_p", bufs=3)
-            nc.vector.tensor_copy(out=zj_p[g][:].bitcast(F32).rearrange("p t (u q) -> p t u q", u=2),
-                                  in_=zj_sb[c][:, 2 * fb:2 * fb + 2, :].bitcast(F32).rearrange("p t (q u) -> p t u q", u=2))
+        def quantize_zj(g):
+            zj_codes[g] = work.tile([P, PAIR_COLS], U32, tag="zj_codes", name="zj_codes", align_bytes=64)
+            zj_scales[g] = work.tile([P, PAIR_COLS], U8, tag="zj_scales", name="zj_scales", align_bytes=64)
+            quantize(zj_codes[g], zj_scales[g], zj_grouped[g])
 
-        def Ac(g, tag="tA"):
-            transposes(("a", g), tag, [word_block(zj_p[g][:, t, :], uk) for t in range(2) for uk in range(2)])
+        def stage1(t):
+            g, cols = t // 2, slice((t % 2) * P, (t % 2 + 1) * P)
+            banks[("rz", t)] = bank("stage1_%d" % (t % 2), STAGE1_PSUM)
+            nc.tensor.matmul_mx(out=banks[("rz", t)][:], lhsT=zj_codes[g][:, cols].bitcast(FP8X4), lhsT_scale=zj_scales[g][:, cols],
+                                rhs=r_codes[:].bitcast(FP8X4), rhs_scale=r_scales[:], start=True, stop=True)
 
-        def Bc(g, eng):
-            zj_g[g] = work.tile([P, 1024], BF16, tag="zj_g", name="zj_g", bufs=PAIRS, align_bytes=64)
-            pair_copy(eng, zj_g[g], banks[("a", g)])
-
-        def Cq(g):
-            zj_c[g] = work.tile([P, 256], U32, tag="zj_c", name="zj_c", bufs=PAIRS, align_bytes=64)
-            zj_s[g] = work.tile([P, 256], U8, tag="zj_s", name="zj_s", bufs=PAIRS, align_bytes=64)
-            quantize(zj_c[g], zj_s[g], zj_g[g])
-
-        def E(t, tag=None):
-            g, et = divmod(t, 2)
-            cols = slice(et * P, (et + 1) * P)
-            banks[("e", t)] = bank(tag or "e%d" % et, BANK_DT)
-            nc.tensor.matmul_mx(out=banks[("e", t)][:], lhsT=zj_c[g][:, cols].bitcast(FP8X4), lhsT_scale=zj_s[g][:, cols],
-                                rhs=r_c[:].bitcast(FP8X4), rhs_scale=r_s[:], start=True, stop=True)
-
-        def Fm(t):
-            g, et = divmod(t, 2)
-            c, f = divmod(t, 4)
-            if et == 0:
+        def multiply_by_zi(t):
+            g = t // 2
+            if t % 2 == 0:
                 p_sb[g] = work.tile([P, 2, H], BF16, tag="p_sb", name="p_sb")
-            nc.vector.tensor_tensor(out=flat_view(p_sb[g][:, et, :]), in0=flat_view(banks[("e", t)][:]), in1=perm_view(zi_sb[c][:, f, :]), op=MULT)
+            nc.vector.tensor_tensor(out=stored_in_transpose_order(p_sb[g][:, t % 2, :]), in0=stored_in_transpose_order(banks[("rz", t)][:]),
+                                    in1=stepped_in_transpose_order(zi_sb[t // 4][:, t % 4, :]), op=MULT)
 
-        def G(g):
-            transposes(("g", g), "tG", [word_block(p_sb[g][:, t, :], u) for t in range(2) for u in range(2)])
+        def transpose_p(g):
+            transpose_four(("p", g), "pT", [word_run(p_sb[g][:, x, :], u) for x in range(2) for u in range(2)])
 
-        def Hc(g, eng):
-            p_g[g] = work.tile([P, 1024], BF16, tag="p_g", name="p_g", align_bytes=64)
-            pair_copy(eng, p_g[g], banks[("g", g)])
+        def copy_p(g):
+            p_grouped[g] = work.tile([P, 4 * PAIR_COLS], BF16, tag="p_grouped", name="p_grouped", align_bytes=64)
+            copy_pair(g == 0, p_grouped[g], banks[("p", g)])
 
-        def Iq(g):
-            p_c[g] = work.tile([P, 256], U32, tag="p_c", name="p_c", align_bytes=64)
-            p_s[g] = work.tile([P, 256], U8, tag="p_s", name="p_s", align_bytes=64)
-            quantize(p_c[g], p_s[g], p_g[g])
+        def quantize_p(g):
+            p_codes[g] = work.tile([P, PAIR_COLS], U32, tag="p_codes", name="p_codes", align_bytes=64)
+            p_scales[g] = work.tile([P, PAIR_COLS], U8, tag="p_scales", name="p_scales", align_bytes=64)
+            quantize(p_codes[g], p_scales[g], p_grouped[g])
 
-        def J(t):
-            g, et = divmod(t, 2)
-            cols = slice(et * P, (et + 1) * P)
-            for n in range(2):
-                banks[("j", t, n)] = bank("j%d" % ((2 * t + n) % 4))
-                nc.tensor.matmul_mx(out=banks[("j", t, n)][:], lhsT=p_c[g][:, cols].bitcast(FP8X4), lhsT_scale=p_s[g][:, cols],
-                                    rhs=d2_c[n][:].bitcast(FP8X4), rhs_scale=d2_s[n][:], start=True, stop=True)
+        def stage2(t):
+            g, cols = t // 2, slice((t % 2) * P, (t % 2 + 1) * P)
+            for half in range(2):
+                banks[("scores", t, half)] = bank("stage2_%d" % ((2 * t + half) % 4))
+                nc.tensor.matmul_mx(out=banks[("scores", t, half)][:], lhsT=p_codes[g][:, cols].bitcast(FP8X4),
+                                    lhsT_scale=p_scales[g][:, cols], rhs=dd_codes[half][:].bitcast(FP8X4),
+                                    rhs_scale=dd_scales[half][:], start=True, stop=True)
 
-        def K(t):
-            c, f = divmod(t, 4)
-            o_sb[t] = work.tile([P, NSE], F32, tag="o_sb", name="o_sb", bufs=6)
-            for n in range(2):
-                half = slice(n * 512, (n + 1) * 512)
-                nc.scalar.activation(out=o_sb[t][:, half], in_=banks[("j", t, n)][:], func=SIGMOID)
-                if t == 2 * PAIRS - 1:
-                    nc.sync.dma_start(out=out_v[c, f][:, half], in_=o_sb[t][:, half])
-            if t < 2 * PAIRS - 1:
-                nc.sync.dma_start(out=out_v[c, f], in_=o_sb[t][:])
+        def sigmoid_and_store(t):
+            result = work.tile([P, NSE], F32, tag="result", name="result", bufs=6)
+            out_rows = out_tiles[t // 4, t % 4]
+            for half in range(2):
+                cols = slice(half * BANK_COLS, (half + 1) * BANK_COLS)
+                nc.scalar.activation(out=result[:, cols], in_=banks[("scores", t, half)][:], func=SIGMOID)
+                if t == LAST_TILE:
+                    nc.sync.dma_start(out=out_rows[:, cols], in_=result[:, cols])
+            if t != LAST_TILE:
+                nc.sync.dma_start(out=out_rows, in_=result[:])
 
-        warm(6)
-        RT(0); RT(1)
-        RC(0, "S"); RC(1, "S")
-        warm(2)
-        DS(0); DS(1)
-        DT(0); DT(1)
-        DC(0, "S"); DC(1, "S")
-        quantize(r_c, r_s, r_g)
-        A(0, "tA"); A(1, "tG")
-        Bc(0, "S"); Bc(1, "S")
-        warm(2)
-        DS(2)
-        Cq(0)
-        DT(2); DC(2, "S")
-        E(0); E(1)
-        DS(3)
-        Cq(1)
-        DT(3); DC(3, "S")
-        Fm(0); Fm(1)
-        G(0)
-        Hc(0, "S")
-        E(2, "j0"); E(3, "j1")
-        DQ(0)
-        Fm(2); Fm(3)
-        A(2, "tA")
-        Bc(2, "S")
-        G(1)
-        Hc(1, "S")
-        A(3, "e1")
-        Bc(3, "S")
-        DQ(1)
-        Iq(0)
-        Cq(2)
-        Iq(1)
-        Pp(4)
-        J(0); J(1)
-        E(4); E(5)
-        K(0); K(1)
-        for s in range(1, PAIRS + 1):
-            if s < PAIRS and s >= 2:
-                G(s)
-            if 4 <= s + 3 < PAIRS:
-                Ac(s + 3)
-            if s + 1 < PAIRS and s + 1 >= 2:
-                Fm(2 * s + 2)
-            if s < PAIRS and s >= 2:
-                Hc(s, "V")
-            if s + 2 < PAIRS and s + 2 >= 3:
-                Cq(s + 2)
-            if s + 1 < PAIRS and s + 1 >= 2:
-                Fm(2 * s + 3)
-            if s < PAIRS and s >= 2:
-                Iq(s)
-            if 4 <= s + 3 < PAIRS:
-                Bc(s + 3, "V")
-            if s + 4 < PAIRS:
-                Pp(s + 4)
-            if s - 1 >= 1:
-                J(2 * s - 2); J(2 * s - 1)
-            if s + 2 < PAIRS and s + 2 >= 3:
-                E(2 * s + 4); E(2 * s + 5)
-            if s - 1 >= 1:
-                K(2 * s - 2); K(2 * s - 1)
+        keep_tensor_clock_up(WARM_UP_MATMULS)
+        for u in range(2):
+            transpose_r(u)
+        for u in range(2):
+            copy_r(u)
+        keep_tensor_clock_up(KEEP_UP_MATMULS)
+        for n in range(2):
+            square_d(n)
+        for n in range(2):
+            transpose_d(n)
+        for n in range(2):
+            copy_d(n)
+        quantize(r_codes, r_scales, r_grouped)
+        transpose_zj(0)
+        transpose_zj(1, "pT")
+        for g in range(2):
+            copy_zj(g)
+        keep_tensor_clock_up(KEEP_UP_MATMULS)
+        square_d(2)
+        quantize_zj(0)
+        transpose_d(2)
+        copy_d(2)
+        stage1(0)
+        stage1(1)
+        square_d(3)
+        quantize_zj(1)
+        transpose_d(3)
+        copy_d(3)
+        multiply_by_zi(0)
+        multiply_by_zi(1)
+        quantize_d(0)
+        quantize_d(1)
+
+        for s in range(PAIRS + 1):
+            if s < PAIRS:
+                transpose_p(s)
+            if s + 2 < PAIRS:
+                transpose_zj(s + 2)
+            if s < PAIRS:
+                copy_p(s)
+            if s + 2 < PAIRS:
+                copy_zj(s + 2)
+            if s + FIRST_REORDERED_PAIR < PAIRS:
+                reorder_zj(s + FIRST_REORDERED_PAIR)
+            if s < PAIRS:
+                quantize_p(s)
+            if s + 1 < PAIRS:
+                stage1(2 * s + 2)
+                stage1(2 * s + 3)
+            if s >= 1:
+                stage2(2 * s - 1)
+            if s < PAIRS:
+                stage2(2 * s)
+            if s + 1 < PAIRS:
+                multiply_by_zi(2 * s + 2)
+                multiply_by_zi(2 * s + 3)
+            if s + 2 < PAIRS:
+                quantize_zj(s + 2)
+            if s >= 1:
+                sigmoid_and_store(2 * s - 1)
+            if s < PAIRS:
+                sigmoid_and_store(2 * s)

from contextlib import ExitStack

import concourse.mybir as mybir
from concourse.masks import make_identity

B, H, NSE = 2048, 512, 1024
FLOPS = 2 * B * H * H + 2 * B * H * NSE

F32 = mybir.dt.float32
BF16 = mybir.dt.bfloat16
U32 = mybir.dt.uint32
U8 = mybir.dt.uint8
FP8X4 = mybir.dt.float8_e4m3fn_x4
MULT = mybir.AluOpType.mult
SIGMOID = mybir.ActivationFunctionType.Sigmoid

P = 128
WORDS = H // 2
QUADS = B // (4 * P)
PAIRS = B // (2 * P)
LAST_TILE = B // P - 1
D_GROUPS = NSE // (2 * P)
BANK_COLS = 512
STAGE1_PSUM = BF16
PAIR_COLS = 2 * P
FIRST_REORDERED_PAIR = 3
WARM_UP_MATMULS = 6
KEEP_UP_MATMULS = 2


def every_second_word(row_tile, u):
    return row_tile.bitcast(F32)[:, u:WORDS:2]


def word_run(row_tile, u):
    return row_tile.bitcast(F32)[:, u * P:(u + 1) * P]


def stepped_in_transpose_order(row_tile):
    return row_tile.rearrange("part (q u e) -> part u q e", u=2, e=2)


def stored_in_transpose_order(row_tile):
    return row_tile.rearrange("part (u q e) -> part u q e", u=2, e=2)


def tile_dedicomdecoder_kernel(tc, z_i, z_j, R, D, out):
    nc = tc.nc
    zj_quads = z_j.rearrange("(c m f) k -> c m f k", m=P, f=4)
    zi_quads = z_i.rearrange("(c m f) h -> c m f h", m=P, f=4)
    out_tiles = out.rearrange("(c m f) r -> c f m r", m=P, f=4)
    r_rows = R.rearrange("(q f) k -> q f k", f=4)
    d_groups = D.rearrange("(n a f) h -> n a f h", a=P, f=2)

    with ExitStack() as ctx:
        keep = ctx.enter_context(tc.tile_pool(name="keep", bufs=1))
        work = ctx.enter_context(tc.tile_pool(name="work", bufs=3))
        psum = ctx.enter_context(tc.psum_pool(name="psum", bufs=1))
        ctx.enter_context(tc.manual_schedule())

        def bank(tag, dtype=F32):
            return psum.tile([P, BANK_COLS], dtype, tag=tag, name=tag)

        zeros = keep.tile([P, BANK_COLS], BF16, tag="zeros", name="zeros")
        nc.vector.memset(zeros[:], 0.0)
        table_in = keep.tile([P, 1], F32, tag="table_in", name="table_in")
        nc.vector.memset(table_in[:], 0.0)
        table_out = keep.tile([P, 1], F32, tag="table_out", name="table_out")
        nc.scalar.activation(out=table_out[:], in_=table_in[:], func=SIGMOID)
        identity = keep.tile([P, P], F32, tag="identity", name="identity")
        make_identity(nc, identity[:])

        r_sb = keep.tile([P, 4, H], BF16, tag="r_sb", name="r_sb")
        d_sb = [keep.tile([P, 2, H], BF16, tag="d_sb%d" % n, name="d_sb%d" % n) for n in range(D_GROUPS)]
        zj_sb = [keep.tile([P, 4, H], BF16, tag="zj_sb%d" % c, name="zj_sb%d" % c) for c in range(QUADS)]
        zi_sb = [keep.tile([P, 4, H], BF16, tag="zi_sb%d" % c, name="zi_sb%d" % c) for c in range(QUADS)]

        def load_d(n):
            nc.sync.dma_start(out=d_sb[n][:], in_=d_groups[n])

        def load_zj(c):
            nc.sync.dma_start(out=zj_sb[c][:], in_=zj_quads[c])

        def load_zi(c):
            nc.sync.dma_start(out=zi_sb[c][:], in_=zi_quads[c])

        nc.sync.dma_start(out=r_sb[:], in_=r_rows)
        load_d(0)
        load_d(1)
        load_zj(0)
        load_d(2)
        load_d(3)
        load_zi(0)
        load_zj(1)
        load_zj(2)
        load_zi(1)
        load_zj(3)
        load_zi(2)
        load_zi(3)

        r_grouped = keep.tile([P, 4 * H], BF16, tag="r_grouped", name="r_grouped", align_bytes=64)
        r_codes = keep.tile([P, H], U32, tag="r_codes", name="r_codes", align_bytes=64)
        r_scales = keep.tile([P, H], U8, tag="r_scales", name="r_scales", align_bytes=64)
        dd_sb = [keep.tile([P, 2, H], BF16, tag="dd_sb%d" % n, name="dd_sb%d" % n) for n in range(D_GROUPS)]
        dd_grouped = [keep.tile([P, 4 * BANK_COLS], BF16, tag="dd_grouped%d" % half, name="dd_grouped%d" % half, align_bytes=64)
                      for half in range(2)]
        dd_codes = [keep.tile([P, BANK_COLS], U32, tag="dd_codes%d" % half, name="dd_codes%d" % half, align_bytes=64)
                    for half in range(2)]
        dd_scales = [keep.tile([P, BANK_COLS], U8, tag="dd_scales%d" % half, name="dd_scales%d" % half, align_bytes=64)
                     for half in range(2)]
        banks, zj_ordered, zj_grouped, zj_codes, zj_scales = {}, {}, {}, {}, {}
        p_sb, p_grouped, p_codes, p_scales = {}, {}, {}, {}

        idle_bank = bank("stage2_3")

        def keep_tensor_clock_up(count):
            for repeat in range(count):
                nc.tensor.matmul(out=idle_bank[:], lhsT=zeros[:, 0:P], rhs=zeros[:], start=True, stop=True)

        def transpose_four(key, tag, sources):
            banks[key] = bank(tag)
            for slot, source in enumerate(sources):
                nc.tensor.transpose(out=banks[key][:, slot * P:(slot + 1) * P], in_=source, identity=identity[:])

        def quantize(codes, scales, grouped):
            nc.vector.quantize_mx(out=codes[:].bitcast(FP8X4), scales=scales[:], in_=grouped[:])

        def transpose_r(u):
            transpose_four(("r", u), "stage1_%d" % u,
                           [every_second_word(r_sb[:, 2 * u + e, :], v) for e in range(2) for v in range(2)])

        def copy_r(u):
            nc.scalar.copy(out=r_grouped[:, u * 2 * H:(u + 1) * 2 * H].bitcast(F32).rearrange("part (q slot) -> part q slot", slot=4),
                           in_=banks[("r", u)][:].rearrange("part (slot q) -> part q slot", slot=4))

        def square_d(n):
            for f in range(2):
                d_rows = stepped_in_transpose_order(d_sb[n][:, f, :])
                nc.vector.tensor_tensor(out=stored_in_transpose_order(dd_sb[n][:, f, :]), in0=d_rows, in1=d_rows, op=MULT)

        def transpose_d(n):
            transpose_four(("d", n), "stage2_%d" % n, [word_run(dd_sb[n][:, f, :], u) for f in range(2) for u in range(2)])

        def copy_d(n):
            cols = slice((n % 2) * 2 * BANK_COLS, (n % 2 + 1) * 2 * BANK_COLS)
            nc.scalar.copy(out=dd_grouped[n // 2][:, cols].bitcast(F32).rearrange("part (a slot) -> part a slot", slot=4),
                           in_=banks[("d", n)][:].rearrange("part (slot a) -> part a slot", slot=4))

        def quantize_d(half):
            quantize(dd_codes[half], dd_scales[half], dd_grouped[half])

        def copy_pair(on_scalar, grouped, pair_bank):
            columns = grouped[:].bitcast(F32).rearrange("part (x m u) -> part x m u", x=2, u=2)
            slots = pair_bank[:].rearrange("part (x u m) -> part x m u", x=2, u=2)
            if on_scalar:
                nc.scalar.copy(out=columns, in_=slots)
            else:
                nc.vector.tensor_copy(out=columns, in_=slots)

        def reorder_zj(g):
            c, first = g // 2, 2 * (g % 2)
            zj_ordered[g] = work.tile([P, 2, H], BF16, tag="zj_ordered", name="zj_ordered")
            nc.vector.tensor_copy(out=zj_ordered[g][:].bitcast(F32).rearrange("part x (u q) -> part x u q", u=2),
                                  in_=zj_sb[c][:, first:first + 2, :].bitcast(F32).rearrange("part x (q u) -> part x u q", u=2))

        def transpose_zj(g, tag="zjT"):
            c, first = g // 2, 2 * (g % 2)
            if g >= FIRST_REORDERED_PAIR:
                sources = [word_run(zj_ordered[g][:, x, :], u) for x in range(2) for u in range(2)]
            else:
                sources = [every_second_word(zj_sb[c][:, first + x, :], u) for x in range(2) for u in range(2)]
            transpose_four(("zj", g), tag, sources)

        def copy_zj(g):
            zj_grouped[g] = work.tile([P, 4 * PAIR_COLS], BF16, tag="zj_grouped", name="zj_grouped", align_bytes=64)
            copy_pair(True, zj_grouped[g], banks[("zj", g)])

        def quantize_zj(g):
            zj_codes[g] = work.tile([P, PAIR_COLS], U32, tag="zj_codes", name="zj_codes", align_bytes=64)
            zj_scales[g] = work.tile([P, PAIR_COLS], U8, tag="zj_scales", name="zj_scales", align_bytes=64)
            quantize(zj_codes[g], zj_scales[g], zj_grouped[g])

        def stage1(t):
            g, cols = t // 2, slice((t % 2) * P, (t % 2 + 1) * P)
            banks[("rz", t)] = bank("stage1_%d" % (t % 2), STAGE1_PSUM)
            nc.tensor.matmul_mx(out=banks[("rz", t)][:], lhsT=zj_codes[g][:, cols].bitcast(FP8X4), lhsT_scale=zj_scales[g][:, cols],
                                rhs=r_codes[:].bitcast(FP8X4), rhs_scale=r_scales[:], start=True, stop=True)

        def multiply_by_zi(t):
            g = t // 2
            if t % 2 == 0:
                p_sb[g] = work.tile([P, 2, H], BF16, tag="p_sb", name="p_sb")
            nc.vector.tensor_tensor(out=stored_in_transpose_order(p_sb[g][:, t % 2, :]), in0=stored_in_transpose_order(banks[("rz", t)][:]),
                                    in1=stepped_in_transpose_order(zi_sb[t // 4][:, t % 4, :]), op=MULT)

        def transpose_p(g):
            transpose_four(("p", g), "pT", [word_run(p_sb[g][:, x, :], u) for x in range(2) for u in range(2)])

        def copy_p(g):
            p_grouped[g] = work.tile([P, 4 * PAIR_COLS], BF16, tag="p_grouped", name="p_grouped", align_bytes=64)
            copy_pair(g == 0, p_grouped[g], banks[("p", g)])

        def quantize_p(g):
            p_codes[g] = work.tile([P, PAIR_COLS], U32, tag="p_codes", name="p_codes", align_bytes=64)
            p_scales[g] = work.tile([P, PAIR_COLS], U8, tag="p_scales", name="p_scales", align_bytes=64)
            quantize(p_codes[g], p_scales[g], p_grouped[g])

        def stage2(t):
            g, cols = t // 2, slice((t % 2) * P, (t % 2 + 1) * P)
            for half in range(2):
                banks[("scores", t, half)] = bank("stage2_%d" % ((2 * t + half) % 4))
                nc.tensor.matmul_mx(out=banks[("scores", t, half)][:], lhsT=p_codes[g][:, cols].bitcast(FP8X4),
                                    lhsT_scale=p_scales[g][:, cols], rhs=dd_codes[half][:].bitcast(FP8X4),
                                    rhs_scale=dd_scales[half][:], start=True, stop=True)

        def sigmoid_and_store(t):
            result = work.tile([P, NSE], F32, tag="result", name="result", bufs=6)
            out_rows = out_tiles[t // 4, t % 4]
            for half in range(2):
                cols = slice(half * BANK_COLS, (half + 1) * BANK_COLS)
                nc.scalar.activation(out=result[:, cols], in_=banks[("scores", t, half)][:], func=SIGMOID)
                if t == LAST_TILE:
                    nc.sync.dma_start(out=out_rows[:, cols], in_=result[:, cols])
            if t != LAST_TILE:
                nc.sync.dma_start(out=out_rows, in_=result[:])

        keep_tensor_clock_up(WARM_UP_MATMULS)
        for u in range(2):
            transpose_r(u)
        for u in range(2):
            copy_r(u)
        keep_tensor_clock_up(KEEP_UP_MATMULS)
        for n in range(2):
            square_d(n)
        for n in range(2):
            transpose_d(n)
        for n in range(2):
            copy_d(n)
        quantize(r_codes, r_scales, r_grouped)
        transpose_zj(0)
        transpose_zj(1, "pT")
        for g in range(2):
            copy_zj(g)
        keep_tensor_clock_up(KEEP_UP_MATMULS)
        square_d(2)
        quantize_zj(0)
        transpose_d(2)
        copy_d(2)
        stage1(0)
        stage1(1)
        square_d(3)
        quantize_zj(1)
        transpose_d(3)
        copy_d(3)
        multiply_by_zi(0)
        multiply_by_zi(1)
        quantize_d(0)
        quantize_d(1)

        for s in range(PAIRS + 1):
            if s < PAIRS:
                transpose_p(s)
            if s + 2 < PAIRS:
                transpose_zj(s + 2)
            if s < PAIRS:
                copy_p(s)
            if s + 2 < PAIRS:
                copy_zj(s + 2)
            if s + FIRST_REORDERED_PAIR < PAIRS:
                reorder_zj(s + FIRST_REORDERED_PAIR)
            if s < PAIRS:
                quantize_p(s)
            if s + 1 < PAIRS:
                stage1(2 * s + 2)
                stage1(2 * s + 3)
            if s >= 1:
                stage2(2 * s - 1)
            if s < PAIRS:
                stage2(2 * s)
            if s + 1 < PAIRS:
                multiply_by_zi(2 * s + 2)
                multiply_by_zi(2 * s + 3)
            if s + 2 < PAIRS:
                quantize_zj(s + 2)
            if s >= 1:
                sigmoid_and_store(2 * s - 1)
            if s < PAIRS:
                sigmoid_and_store(2 * s)
